import numpy as np
import ml_dtypes

BF16 = ml_dtypes.bfloat16


def bf(x):
    return np.asarray(x, np.float32).astype(BF16)


def f32(x):
    return np.asarray(x, np.float32)


def f64(x):
    return np.asarray(x).astype(np.float64)


def striped(idx):
    return np.tile(idx.reshape(-1, 16).T, (8, 1))


S, D, M, H, O, F, B, N = 4096, 128, 128, 128, 128, 8, 512, 4096


def setup_inputs():
    return {"table": bf(np.random.standard_normal((D, S)) / np.sqrt(F)), "w1": bf(np.random.standard_normal((D, M)) / np.sqrt(D)), "b1": f32(0.2 * np.random.standard_normal((M, 1))), "w2": bf(np.random.standard_normal((M, H)) * np.sqrt(2.0 / M)), "b2": f32(0.2 * np.random.standard_normal((H, 1))), "w3": bf(np.random.standard_normal((H, O)) * np.sqrt(2.0 / H)), "b3": f32(0.2 * np.random.standard_normal((O, 1))), "offs": striped(np.random.permutation(np.tile(np.arange(S), 2))[:N])}


def reference(table, w1, b1, w2, b2, w3, b3, offs):
    idx = offs[:16].T.reshape(-1)
    y = f64(w1).T @ f64(table)[:, idx]
    acc = y.reshape(M, F, B).sum(axis=1)
    h1 = np.maximum(acc + f64(b1), 0.0)
    h2 = np.maximum(f64(w2).T @ h1 + f64(b2), 0.0)
    return np.tanh(f64(w3).T @ h2 + f64(b3))

@@ -1,0 +1,50 @@
+import concourse.mybir as mybir
+
+BF16, F32, U16 = mybir.dt.bfloat16, mybir.dt.float32, mybir.dt.uint16
+RELU = mybir.ActivationFunctionType.Relu
+TANH = mybir.ActivationFunctionType.Tanh
+
+P = 128
+S = 4096
+SLOTS = 8
+B = 512
+N = SLOTS * B
+COLS = B // 16
+
+FLOPS = 2 * P * P * N + 2 * (2 * P * P * B)
+
+
+def tile_nnuemodel_kernel(tc, table, w1, b1, w2, b2, w3, b3, offs, out):
+    nc = tc.nc
+    with tc.tile_pool(name="held", bufs=1) as held, tc.psum_pool(name="psum", bufs=1) as psum:
+        offsets = held.tile([P, N // 16], U16, name="offsets")
+        nc.sync.dma_start(offsets[:], offs)
+        table_sb = held.tile([P, S], BF16, name="table_sb")
+        nc.sync.dma_start(table_sb[:], table)
+
+        w1_sb = held.tile([P, P], BF16, name="w1_sb")
+        w2_sb = held.tile([P, P], BF16, name="w2_sb")
+        w3_sb = held.tile([P, P], BF16, name="w3_sb")
+        b1_sb = held.tile([P, 1], F32, name="b1_sb")
+        b2_sb = held.tile([P, 1], F32, name="b2_sb")
+        b3_sb = held.tile([P, 1], F32, name="b3_sb")
+        for tile_sb, dram in ((w1_sb, w1), (b1_sb, b1), (w2_sb, w2), (b2_sb, b2), (w3_sb, w3), (b3_sb, b3)):
+            nc.scalar.dma_start(tile_sb[:], dram)
+
+        acc = psum.tile([P, B], F32, name="acc")
+        for t in range(SLOTS):
+            picked = table_sb[:].indirect(offsets[:, t * COLS : (t + 1) * COLS])
+            nc.tensor.matmul(acc[:], w1_sb[:], picked, start=(t == 0), stop=(t == SLOTS - 1))
+        h1 = held.tile([P, B], BF16, name="h1")
+        nc.scalar.activation(h1[:], acc[:], RELU, bias=b1_sb[:])
+
+        z2 = psum.tile([P, B], F32, name="z2")
+        nc.tensor.matmul(z2[:], w2_sb[:], h1[:], start=True, stop=True)
+        h2 = held.tile([P, B], BF16, name="h2")
+        nc.scalar.activation(h2[:], z2[:], RELU, bias=b2_sb[:])
+
+        z3 = psum.tile([P, B], F32, name="z3")
+        nc.tensor.matmul(z3[:], w3_sb[:], h2[:], start=True, stop=True)
+        y = held.tile([P, B], F32, name="y")
+        nc.scalar.activation(y[:], z3[:], TANH, bias=b3_sb[:])
+        nc.sync.dma_start(out, y[:])

@@ -10,6 +10,7 @@ SLOTS = 8
 B = 512
 N = SLOTS * B
 COLS = B // 16
+WARM = 10
 
 FLOPS = 2 * P * P * N + 2 * (2 * P * P * B)
 
@@ -30,6 +31,12 @@ def tile_nnuemodel_kernel(tc, table, w1, b1, w2, b2, w3, b3, offs, out):
         b3_sb = held.tile([P, 1], F32, name="b3_sb")
         for tile_sb, dram in ((w1_sb, w1), (b1_sb, b1), (w2_sb, w2), (b2_sb, b2), (w3_sb, w3), (b3_sb, b3)):
             nc.scalar.dma_start(tile_sb[:], dram)
+
+        zeros = held.tile([P, B], BF16, name="zeros")
+        nc.vector.memset(zeros[:], 0.0)
+        idle = psum.tile([P, B], F32, name="idle")
+        for k in range(WARM):
+            nc.tensor.matmul(idle[:], zeros[:, 0:P], zeros[:], start=True, stop=True)
 
         acc = psum.tile([P, B], F32, name="acc")
         for t in range(SLOTS):

@@ -3,6 +3,7 @@ import concourse.mybir as mybir
 BF16, F32, U16 = mybir.dt.bfloat16, mybir.dt.float32, mybir.dt.uint16
 RELU = mybir.ActivationFunctionType.Relu
 TANH = mybir.ActivationFunctionType.Tanh
+ADD, MAX = mybir.AluOpType.add, mybir.AluOpType.max
 
 P = 128
 S = 4096
@@ -10,7 +11,7 @@ SLOTS = 8
 B = 512
 N = SLOTS * B
 COLS = B // 16
-WARM = 10
+HALF = B // 2
 
 FLOPS = 2 * P * P * N + 2 * (2 * P * P * B)
 
@@ -32,26 +33,24 @@ def tile_nnuemodel_kernel(tc, table, w1, b1, w2, b2, w3, b3, offs, out):
         for tile_sb, dram in ((w1_sb, w1), (b1_sb, b1), (w2_sb, w2), (b2_sb, b2), (w3_sb, w3), (b3_sb, b3)):
             nc.scalar.dma_start(tile_sb[:], dram)
 
-        zeros = held.tile([P, B], BF16, name="zeros")
-        nc.vector.memset(zeros[:], 0.0)
-        idle = psum.tile([P, B], F32, name="idle")
-        for k in range(WARM):
-            nc.tensor.matmul(idle[:], zeros[:, 0:P], zeros[:], start=True, stop=True)
-
         acc = psum.tile([P, B], F32, name="acc")
         for t in range(SLOTS):
             picked = table_sb[:].indirect(offsets[:, t * COLS : (t + 1) * COLS])
             nc.tensor.matmul(acc[:], w1_sb[:], picked, start=(t == 0), stop=(t == SLOTS - 1))
-        h1 = held.tile([P, B], BF16, name="h1")
-        nc.scalar.activation(h1[:], acc[:], RELU, bias=b1_sb[:])
 
-        z2 = psum.tile([P, B], F32, name="z2")
-        nc.tensor.matmul(z2[:], w2_sb[:], h1[:], start=True, stop=True)
-        h2 = held.tile([P, B], BF16, name="h2")
-        nc.scalar.activation(h2[:], z2[:], RELU, bias=b2_sb[:])
-
-        z3 = psum.tile([P, B], F32, name="z3")
-        nc.tensor.matmul(z3[:], w3_sb[:], h2[:], start=True, stop=True)
-        y = held.tile([P, B], F32, name="y")
-        nc.scalar.activation(y[:], z3[:], TANH, bias=b3_sb[:])
-        nc.sync.dma_start(out, y[:])
+        halves = [slice(i * HALF, (i + 1) * HALF) for i in range(2)]
+        h1 = [held.tile([P, HALF], BF16, name=f"h1_{i}") for i in range(2)]
+        z2 = [psum.tile([P, HALF], F32, name=f"z2_{i}") for i in range(2)]
+        h2 = [held.tile([P, HALF], BF16, name=f"h2_{i}") for i in range(2)]
+        z3 = [psum.tile([P, HALF], F32, name=f"z3_{i}") for i in range(2)]
+        y = [held.tile([P, HALF], F32, name=f"y_{i}") for i in range(2)]
+        for i in range(2):
+            nc.scalar.activation(h1[i][:], acc[:, halves[i]], RELU, bias=b1_sb[:])
+        for i in range(2):
+            nc.tensor.matmul(z2[i][:], w2_sb[:], h1[i][:], start=True, stop=True)
+            nc.vector.tensor_scalar(h2[i][:], z2[i][:], b2_sb[:], 0.0, ADD, MAX)
+        for i in range(2):
+            nc.tensor.matmul(z3[i][:], w3_sb[:], h2[i][:], start=True, stop=True)
+            nc.scalar.activation(y[i][:], z3[i][:], TANH, bias=b3_sb[:])
+        nc.sync.dma_start(out[:, halves[0]], y[0][:])
+        nc.scalar.dma_start(out[:, halves[1]], y[1][:])

@@ -21,17 +21,18 @@ def tile_nnuemodel_kernel(tc, table, w1, b1, w2, b2, w3, b3, offs, out):
     with tc.tile_pool(name="held", bufs=1) as held, tc.psum_pool(name="psum", bufs=1) as psum:
         offsets = held.tile([P, N // 16], U16, name="offsets")
         nc.sync.dma_start(offsets[:], offs)
+        w1_sb = held.tile([P, P], BF16, name="w1_sb")
+        nc.scalar.dma_start(w1_sb[:], w1)
         table_sb = held.tile([P, S], BF16, name="table_sb")
         nc.sync.dma_start(table_sb[:], table)
 
-        w1_sb = held.tile([P, P], BF16, name="w1_sb")
         w2_sb = held.tile([P, P], BF16, name="w2_sb")
         w3_sb = held.tile([P, P], BF16, name="w3_sb")
         b1_sb = held.tile([P, 1], F32, name="b1_sb")
         b2_sb = held.tile([P, 1], F32, name="b2_sb")
         b3_sb = held.tile([P, 1], F32, name="b3_sb")
-        for tile_sb, dram in ((w1_sb, w1), (b1_sb, b1), (w2_sb, w2), (b2_sb, b2), (w3_sb, w3), (b3_sb, b3)):
-            nc.scalar.dma_start(tile_sb[:], dram)
+        for tile_sb, dram in ((b1_sb, b1), (w2_sb, w2), (b2_sb, b2), (w3_sb, w3), (b3_sb, b3)):
+            nc.sync.dma_start(tile_sb[:], dram)
 
         acc = psum.tile([P, B], F32, name="acc")
         for t in range(SLOTS):

@@ -12,6 +12,7 @@ B = 512
 N = SLOTS * B
 COLS = B // 16
 HALF = B // 2
+WARM = 16
 
 FLOPS = 2 * P * P * N + 2 * (2 * P * P * B)
 
@@ -33,6 +34,12 @@ def tile_nnuemodel_kernel(tc, table, w1, b1, w2, b2, w3, b3, offs, out):
         b3_sb = held.tile([P, 1], F32, name="b3_sb")
         for tile_sb, dram in ((b1_sb, b1), (w2_sb, w2), (b2_sb, b2), (w3_sb, w3), (b3_sb, b3)):
             nc.sync.dma_start(tile_sb[:], dram)
+
+        zeros = held.tile([P, B], BF16, name="zeros")
+        nc.vector.memset(zeros[:], 0.0)
+        idle = psum.tile([P, B], F32, name="idle")
+        for k in range(WARM):
+            nc.tensor.matmul(idle[:], zeros[:, 0:P], zeros[:], start=True, stop=True)
 
         acc = psum.tile([P, B], F32, name="acc")
         for t in range(SLOTS):

@@ -12,7 +12,6 @@ B = 512
 N = SLOTS * B
 COLS = B // 16
 HALF = B // 2
-WARM = 16
 
 FLOPS = 2 * P * P * N + 2 * (2 * P * P * B)
 
@@ -25,7 +24,8 @@ def tile_nnuemodel_kernel(tc, table, w1, b1, w2, b2, w3, b3, offs, out):
         w1_sb = held.tile([P, P], BF16, name="w1_sb")
         nc.scalar.dma_start(w1_sb[:], w1)
         table_sb = held.tile([P, S], BF16, name="table_sb")
-        nc.sync.dma_start(table_sb[:], table)
+        nc.sync.dma_start(table_sb[:, 0 : S // 2], table[:, 0 : S // 2])
+        nc.scalar.dma_start(table_sb[:, S // 2 : S], table[:, S // 2 : S])
 
         w2_sb = held.tile([P, P], BF16, name="w2_sb")
         w3_sb = held.tile([P, P], BF16, name="w3_sb")
@@ -34,12 +34,6 @@ def tile_nnuemodel_kernel(tc, table, w1, b1, w2, b2, w3, b3, offs, out):
         b3_sb = held.tile([P, 1], F32, name="b3_sb")
         for tile_sb, dram in ((b1_sb, b1), (w2_sb, w2), (b2_sb, b2), (w3_sb, w3), (b3_sb, b3)):
             nc.sync.dma_start(tile_sb[:], dram)
-
-        zeros = held.tile([P, B], BF16, name="zeros")
-        nc.vector.memset(zeros[:], 0.0)
-        idle = psum.tile([P, B], F32, name="idle")
-        for k in range(WARM):
-            nc.tensor.matmul(idle[:], zeros[:, 0:P], zeros[:], start=True, stop=True)
 
         acc = psum.tile([P, B], F32, name="acc")
         for t in range(SLOTS):

@@ -1,7 +1,6 @@
 import concourse.mybir as mybir
 
 BF16, F32, U16 = mybir.dt.bfloat16, mybir.dt.float32, mybir.dt.uint16
-RELU = mybir.ActivationFunctionType.Relu
 TANH = mybir.ActivationFunctionType.Tanh
 ADD, MAX = mybir.AluOpType.add, mybir.AluOpType.max
 
@@ -47,7 +46,7 @@ def tile_nnuemodel_kernel(tc, table, w1, b1, w2, b2, w3, b3, offs, out):
         z3 = [psum.tile([P, HALF], F32, name=f"z3_{i}") for i in range(2)]
         y = [held.tile([P, HALF], F32, name=f"y_{i}") for i in range(2)]
         for i in range(2):
-            nc.scalar.activation(h1[i][:], acc[:, halves[i]], RELU, bias=b1_sb[:])
+            nc.vector.tensor_scalar(h1[i][:], acc[:, halves[i]], b1_sb[:], 0.0, ADD, MAX)
         for i in range(2):
             nc.tensor.matmul(z2[i][:], w2_sb[:], h1[i][:], start=True, stop=True)
             nc.vector.tensor_scalar(h2[i][:], z2[i][:], b2_sb[:], 0.0, ADD, MAX)

@@ -10,7 +10,8 @@ SLOTS = 8
 B = 512
 N = SLOTS * B
 COLS = B // 16
-HALF = B // 2
+PIECES = 4
+W = B // PIECES
 
 FLOPS = 2 * P * P * N + 2 * (2 * P * P * B)
 
@@ -39,19 +40,18 @@ def tile_nnuemodel_kernel(tc, table, w1, b1, w2, b2, w3, b3, offs, out):
             picked = table_sb[:].indirect(offsets[:, t * COLS : (t + 1) * COLS])
             nc.tensor.matmul(acc[:], w1_sb[:], picked, start=(t == 0), stop=(t == SLOTS - 1))
 
-        halves = [slice(i * HALF, (i + 1) * HALF) for i in range(2)]
-        h1 = [held.tile([P, HALF], BF16, name=f"h1_{i}") for i in range(2)]
-        z2 = [psum.tile([P, HALF], F32, name=f"z2_{i}") for i in range(2)]
-        h2 = [held.tile([P, HALF], BF16, name=f"h2_{i}") for i in range(2)]
-        z3 = [psum.tile([P, HALF], F32, name=f"z3_{i}") for i in range(2)]
-        y = [held.tile([P, HALF], F32, name=f"y_{i}") for i in range(2)]
-        for i in range(2):
-            nc.vector.tensor_scalar(h1[i][:], acc[:, halves[i]], b1_sb[:], 0.0, ADD, MAX)
-        for i in range(2):
-            nc.tensor.matmul(z2[i][:], w2_sb[:], h1[i][:], start=True, stop=True)
-            nc.vector.tensor_scalar(h2[i][:], z2[i][:], b2_sb[:], 0.0, ADD, MAX)
-        for i in range(2):
+        cols = [slice(i * W, (i + 1) * W) for i in range(PIECES)]
+        h1 = [held.tile([P, W], BF16, name=f"h1_{i}") for i in range(PIECES)]
+        z2 = [psum.tile([P, W], F32, name=f"z2_{i}") for i in range(2)]
+        h2 = [held.tile([P, W], BF16, name=f"h2_{i}") for i in range(PIECES)]
+        z3 = [psum.tile([P, W], F32, name=f"z3_{i}") for i in range(PIECES)]
+        y = [held.tile([P, W], F32, name=f"y_{i}") for i in range(PIECES)]
+        for i in range(PIECES):
+            nc.vector.tensor_scalar(h1[i][:], acc[:, cols[i]], b1_sb[:], 0.0, ADD, MAX)
+        for i in range(PIECES):
+            nc.tensor.matmul(z2[i % 2][:], w2_sb[:], h1[i][:], start=True, stop=True)
+            nc.vector.tensor_scalar(h2[i][:], z2[i % 2][:], b2_sb[:], 0.0, ADD, MAX)
+        for i in range(PIECES):
             nc.tensor.matmul(z3[i][:], w3_sb[:], h2[i][:], start=True, stop=True)
             nc.scalar.activation(y[i][:], z3[i][:], TANH, bias=b3_sb[:])
-        nc.sync.dma_start(out[:, halves[0]], y[0][:])
-        nc.scalar.dma_start(out[:, halves[1]], y[1][:])
+            nc.sync.dma_start(out[:, cols[i]], y[i][:])

@@ -35,22 +35,23 @@ def tile_nnuemodel_kernel(tc, table, w1, b1, w2, b2, w3, b3, offs, out):
         for tile_sb, dram in ((b1_sb, b1), (w2_sb, w2), (b2_sb, b2), (w3_sb, w3), (b3_sb, b3)):
             nc.sync.dma_start(tile_sb[:], dram)
 
-        acc = psum.tile([P, B], F32, name="acc")
+        acc = psum.tile([P, B], F32, name="acc", tag="acc")
         for t in range(SLOTS):
             picked = table_sb[:].indirect(offsets[:, t * COLS : (t + 1) * COLS])
             nc.tensor.matmul(acc[:], w1_sb[:], picked, start=(t == 0), stop=(t == SLOTS - 1))
 
         cols = [slice(i * W, (i + 1) * W) for i in range(PIECES)]
         h1 = [held.tile([P, W], BF16, name=f"h1_{i}") for i in range(PIECES)]
-        z2 = [psum.tile([P, W], F32, name=f"z2_{i}") for i in range(2)]
+        z2 = [psum.tile([P, W], F32, name=f"z2_{i}") for i in range(PIECES)]
         h2 = [held.tile([P, W], BF16, name=f"h2_{i}") for i in range(PIECES)]
-        z3 = [psum.tile([P, W], F32, name=f"z3_{i}") for i in range(PIECES)]
+        z3 = [psum.tile([P, W], F32, name=f"z3_{i}") for i in range(PIECES - 1)]
         y = [held.tile([P, W], F32, name=f"y_{i}") for i in range(PIECES)]
         for i in range(PIECES):
             nc.vector.tensor_scalar(h1[i][:], acc[:, cols[i]], b1_sb[:], 0.0, ADD, MAX)
+        z3.append(psum.tile([P, W], F32, name=f"z3_{PIECES - 1}", tag="acc"))
         for i in range(PIECES):
-            nc.tensor.matmul(z2[i % 2][:], w2_sb[:], h1[i][:], start=True, stop=True)
-            nc.vector.tensor_scalar(h2[i][:], z2[i % 2][:], b2_sb[:], 0.0, ADD, MAX)
+            nc.tensor.matmul(z2[i][:], w2_sb[:], h1[i][:], start=True, stop=True)
+            nc.vector.tensor_scalar(h2[i][:], z2[i][:], b2_sb[:], 0.0, ADD, MAX)
         for i in range(PIECES):
             nc.tensor.matmul(z3[i][:], w3_sb[:], h2[i][:], start=True, stop=True)
             nc.scalar.activation(y[i][:], z3[i][:], TANH, bias=b3_sb[:])

@@ -55,4 +55,5 @@ def tile_nnuemodel_kernel(tc, table, w1, b1, w2, b2, w3, b3, offs, out):
         for i in range(PIECES):
             nc.tensor.matmul(z3[i][:], w3_sb[:], h2[i][:], start=True, stop=True)
             nc.scalar.activation(y[i][:], z3[i][:], TANH, bias=b3_sb[:])
-            nc.sync.dma_start(out[:, cols[i]], y[i][:])
+            store_queue = nc.scalar if i == PIECES - 1 else nc.sync
+            store_queue.dma_start(out[:, cols[i]], y[i][:])

@@ -21,11 +21,11 @@ def tile_nnuemodel_kernel(tc, table, w1, b1, w2, b2, w3, b3, offs, out):
     with tc.tile_pool(name="held", bufs=1) as held, tc.psum_pool(name="psum", bufs=1) as psum:
         offsets = held.tile([P, N // 16], U16, name="offsets")
         nc.sync.dma_start(offsets[:], offs)
-        w1_sb = held.tile([P, P], BF16, name="w1_sb")
-        nc.scalar.dma_start(w1_sb[:], w1)
         table_sb = held.tile([P, S], BF16, name="table_sb")
         nc.sync.dma_start(table_sb[:, 0 : S // 2], table[:, 0 : S // 2])
         nc.scalar.dma_start(table_sb[:, S // 2 : S], table[:, S // 2 : S])
+        w1_sb = held.tile([P, P], BF16, name="w1_sb")
+        nc.scalar.dma_start(w1_sb[:], w1)
 
         w2_sb = held.tile([P, P], BF16, name="w2_sb")
         w3_sb = held.tile([P, P], BF16, name="w3_sb")

@@ -32,7 +32,7 @@ def tile_nnuemodel_kernel(tc, table, w1, b1, w2, b2, w3, b3, offs, out):
         b1_sb = held.tile([P, 1], F32, name="b1_sb")
         b2_sb = held.tile([P, 1], F32, name="b2_sb")
         b3_sb = held.tile([P, 1], F32, name="b3_sb")
-        for tile_sb, dram in ((b1_sb, b1), (w2_sb, w2), (b2_sb, b2), (w3_sb, w3), (b3_sb, b3)):
+        for tile_sb, dram in ((w2_sb, w2), (w3_sb, w3), (b1_sb, b1), (b2_sb, b2), (b3_sb, b3)):
             nc.sync.dma_start(tile_sb[:], dram)
 
         acc = psum.tile([P, B], F32, name="acc", tag="acc")

@@ -22,10 +22,10 @@ def tile_nnuemodel_kernel(tc, table, w1, b1, w2, b2, w3, b3, offs, out):
         offsets = held.tile([P, N // 16], U16, name="offsets")
         nc.sync.dma_start(offsets[:], offs)
         table_sb = held.tile([P, S], BF16, name="table_sb")
-        nc.sync.dma_start(table_sb[:, 0 : S // 2], table[:, 0 : S // 2])
-        nc.scalar.dma_start(table_sb[:, S // 2 : S], table[:, S // 2 : S])
         w1_sb = held.tile([P, P], BF16, name="w1_sb")
+        nc.scalar.dma_start(table_sb[:, S // 2 : S], table[:, S // 2 : S])
         nc.scalar.dma_start(w1_sb[:], w1)
+        nc.sync.dma_start(table_sb[:, 0 : S // 2], table[:, 0 : S // 2])
 
         w2_sb = held.tile([P, P], BF16, name="w2_sb")
         w3_sb = held.tile([P, P], BF16, name="w3_sb")

import concourse.mybir as mybir

BF16, F32, U16 = mybir.dt.bfloat16, mybir.dt.float32, mybir.dt.uint16
TANH = mybir.ActivationFunctionType.Tanh
ADD, MAX = mybir.AluOpType.add, mybir.AluOpType.max

P = 128
S = 4096
SLOTS = 8
B = 512
N = SLOTS * B
COLS = B // 16
PIECES = 4
W = B // PIECES

FLOPS = 2 * P * P * N + 2 * (2 * P * P * B)


def tile_nnuemodel_kernel(tc, table, w1, b1, w2, b2, w3, b3, offs, out):
    nc = tc.nc
    with tc.tile_pool(name="held", bufs=1) as held, tc.psum_pool(name="psum", bufs=1) as psum:
        offsets = held.tile([P, N // 16], U16, name="offsets")
        nc.sync.dma_start(offsets[:], offs)
        table_sb = held.tile([P, S], BF16, name="table_sb")
        w1_sb = held.tile([P, P], BF16, name="w1_sb")
        nc.scalar.dma_start(table_sb[:, S // 2 : S], table[:, S // 2 : S])
        nc.scalar.dma_start(w1_sb[:], w1)
        nc.sync.dma_start(table_sb[:, 0 : S // 2], table[:, 0 : S // 2])

        w2_sb = held.tile([P, P], BF16, name="w2_sb")
        w3_sb = held.tile([P, P], BF16, name="w3_sb")
        b1_sb = held.tile([P, 1], F32, name="b1_sb")
        b2_sb = held.tile([P, 1], F32, name="b2_sb")
        b3_sb = held.tile([P, 1], F32, name="b3_sb")
        for tile_sb, dram in ((w2_sb, w2), (w3_sb, w3), (b1_sb, b1), (b2_sb, b2), (b3_sb, b3)):
            nc.sync.dma_start(tile_sb[:], dram)

        acc = psum.tile([P, B], F32, name="acc", tag="acc")
        for t in range(SLOTS):
            picked = table_sb[:].indirect(offsets[:, t * COLS : (t + 1) * COLS])
            nc.tensor.matmul(acc[:], w1_sb[:], picked, start=(t == 0), stop=(t == SLOTS - 1))

        cols = [slice(i * W, (i + 1) * W) for i in range(PIECES)]
        h1 = [held.tile([P, W], BF16, name=f"h1_{i}") for i in range(PIECES)]
        z2 = [psum.tile([P, W], F32, name=f"z2_{i}") for i in range(PIECES)]
        h2 = [held.tile([P, W], BF16, name=f"h2_{i}") for i in range(PIECES)]
        z3 = [psum.tile([P, W], F32, name=f"z3_{i}") for i in range(PIECES - 1)]
        y = [held.tile([P, W], F32, name=f"y_{i}") for i in range(PIECES)]
        for i in range(PIECES):
            nc.vector.tensor_scalar(h1[i][:], acc[:, cols[i]], b1_sb[:], 0.0, ADD, MAX)
        z3.append(psum.tile([P, W], F32, name=f"z3_{PIECES - 1}", tag="acc"))
        for i in range(PIECES):
            nc.tensor.matmul(z2[i][:], w2_sb[:], h1[i][:], start=True, stop=True)
            nc.vector.tensor_scalar(h2[i][:], z2[i][:], b2_sb[:], 0.0, ADD, MAX)
        for i in range(PIECES):
            nc.tensor.matmul(z3[i][:], w3_sb[:], h2[i][:], start=True, stop=True)
            nc.scalar.activation(y[i][:], z3[i][:], TANH, bias=b3_sb[:])
            store_queue = nc.scalar if i == PIECES - 1 else nc.sync
            store_queue.dma_start(out[:, cols[i]], y[i][:])
